import numpy as np
import ml_dtypes


def mxq(x, axis, fmt="e4m3"):
    dtype, down = {"e4m3": (ml_dtypes.float8_e4m3fn, 7), "e5m2": (ml_dtypes.float8_e5m2, 14)}[fmt]
    v = np.moveaxis(np.asarray(x, np.float32).astype(ml_dtypes.bfloat16).astype(np.float64), axis, -1)
    blocks = v.reshape(v.shape[:-1] + (-1, 32))
    amax = np.abs(blocks).max(-1, keepdims=True)
    byte = np.maximum(np.where(amax > 0, np.frexp(amax)[1] - 1 + 127, 0) - down, 1)
    scale = np.exp2(byte - 127.0)
    codes = (blocks / scale).astype(np.float32).astype(dtype).astype(np.float64)
    return np.moveaxis((codes * scale).reshape(v.shape), -1, axis)


WIDE = False


def mx_kscale(k):
    if not WIDE:
        return np.ones(k)
    levels = np.array([10, -10, 5, -5, 0])
    a = np.random.permutation(np.resize(levels, k // 512 * 4)).reshape(k // 512, 4)
    idx = np.arange(k)
    return np.exp2(a[idx // 512, idx % 128 // 32])


BF16 = ml_dtypes.bfloat16


def bf(x):
    return np.asarray(x, np.float32).astype(BF16)


def f64(x):
    return np.asarray(x).astype(np.float64)


B, N_IN, N_OUT, D_IN, D_OUT = 128, 4, 16, 8192, 16


def setup_inputs():
    s = mx_kscale(D_IN)
    inputs = np.random.standard_normal((B, N_IN, D_IN, 1)) * s[:, None]
    transform_mat = np.random.uniform(-1.0, 1.0, (1, N_IN, N_OUT, D_IN, D_OUT, 1)) * np.sqrt(3.0 / D_IN) / s[:, None, None]
    return {"inputs": bf(inputs), "transform_mat": bf(transform_mat)}


def reference(inputs, transform_mat):
    xq = mxq(f64(inputs)[..., 0], 2, "e4m3")
    wq = mxq(f64(transform_mat)[0, ..., 0], 2, "e4m3")
    prod = xq.transpose(1, 0, 2) @ wq.transpose(0, 2, 1, 3).reshape(N_IN, D_IN, N_OUT * D_OUT)
    votes = prod.reshape(N_IN, B, N_OUT, D_OUT).transpose(1, 0, 2, 3)
    return votes[..., None]

@@ -1,0 +1,131 @@
+from contextlib import ExitStack
+
+import concourse.mybir as mybir
+from concourse.masks import make_identity
+
+BF16 = mybir.dt.bfloat16
+F32 = mybir.dt.float32
+U32 = mybir.dt.uint32
+U8 = mybir.dt.uint8
+FP8X4 = mybir.dt.float8_e4m3fn_x4
+
+P = 128
+BATCH = 128
+CAPS_IN = 4
+CAPS_OUT = 16
+D_IN = 8192
+D_OUT = 16
+COLS = CAPS_OUT * D_OUT
+
+PACK = 4
+GROUPS = 4
+RUN = GROUPS * PACK
+HALVES = 2
+CLASSES = 4
+CHUNKS = D_IN // (CLASSES * HALVES * RUN)
+WORDS_OF_RUN = RUN // 2
+VECTOR_GROUPS = 2
+
+FLOPS = 2 * BATCH * CAPS_IN * D_IN * COLS
+
+
+def tile_transforming_k_kernel(tc, inputs, transform_mat, out):
+    nc = tc.nc
+    assert CHUNKS * HALVES == P
+
+    x_dram = inputs.rearrange("b n i one -> b n (i one)")
+    w_dram = transform_mat.rearrange(
+        "one n m (j c h r) o uno -> (one n) c h j m (r o uno)", j=CHUNKS, c=CLASSES, h=HALVES, r=RUN
+    )
+    out_dram = out.rearrange("b n m o one -> b n (m o one)")
+
+    with ExitStack() as ctx:
+        keep = ctx.enter_context(tc.tile_pool(name="keep", bufs=1))
+        x_in = ctx.enter_context(tc.tile_pool(name="x_in", bufs=CAPS_IN))
+        x_mid = ctx.enter_context(tc.tile_pool(name="x_mid", bufs=3))
+        w_in = ctx.enter_context(tc.tile_pool(name="w_in", bufs=6))
+        w_mid = ctx.enter_context(tc.tile_pool(name="w_mid", bufs=3))
+        results = ctx.enter_context(tc.tile_pool(name="results", bufs=2))
+        psum_t = ctx.enter_context(tc.psum_pool(name="psum_t", bufs=4))
+        psum_acc = ctx.enter_context(tc.psum_pool(name="psum_acc", bufs=2))
+
+        ident = keep.tile([P, P], F32)
+        make_identity(nc, ident[:])
+
+        x_codes = keep.tile([P, CAPS_IN, CLASSES, GROUPS * BATCH], U32, align_bytes=64)
+        x_scales = keep.tile([P, CAPS_IN, CLASSES, GROUPS * BATCH], U8, align_bytes=64)
+
+        for n in range(CAPS_IN):
+            x_rows = x_in.tile([P, D_IN], BF16)
+            nc.sync.dma_start(out=x_rows[:], in_=x_dram[:, n, :])
+            by_class = x_rows[:].rearrange("b (j c s) -> b c j s", c=CLASSES, s=HALVES * RUN)
+            for c in range(CLASSES):
+                x_sorted = x_mid.tile([P, P * RUN], BF16)
+                nc.vector.tensor_copy(
+                    out=x_sorted[:].rearrange("b (j s) -> b j s", s=HALVES * RUN),
+                    in_=by_class[:, c],
+                )
+                x_words = x_sorted[:].bitcast(F32).rearrange("b (p w) -> b p w", w=WORDS_OF_RUN)
+                x_grouped = x_mid.tile([P, GROUPS * BATCH * PACK], BF16, align_bytes=64)
+                grouped_words = x_grouped[:].bitcast(F32).rearrange(
+                    "p (g b u) -> p g b u", g=GROUPS, b=BATCH
+                )
+                for first_g in range(0, GROUPS, 2):
+                    xt = psum_t.tile([P, 4 * BATCH], F32)
+                    for w in range(4):
+                        nc.tensor.transpose(
+                            xt[:, w * BATCH : (w + 1) * BATCH],
+                            x_words[:, :, 2 * first_g + w],
+                            ident[:],
+                        )
+                    nc.scalar.copy(
+                        out=grouped_words[:, first_g : first_g + 2],
+                        in_=xt[:].rearrange("p (g u b) -> p g b u", g=2, u=2),
+                    )
+                nc.vector.quantize_mx(
+                    out=x_codes[:, n, c, :].bitcast(FP8X4),
+                    scales=x_scales[:, n, c, :],
+                    in_=x_grouped[:],
+                )
+
+        for n in range(CAPS_IN):
+            acc = psum_acc.tile([P, COLS], F32)
+            for c in range(CLASSES):
+                w_rows = w_in.tile([P, CAPS_OUT * RUN * D_OUT], BF16)
+                for h in range(HALVES):
+                    nc.sync.dma_start(
+                        out=w_rows[h:P:HALVES, :].rearrange("p (m e) -> p m e", m=CAPS_OUT),
+                        in_=w_dram[n, c, h],
+                    )
+                w_grouped = w_mid.tile([P, GROUPS * COLS * PACK], BF16, align_bytes=64)
+                src = w_rows[:].rearrange(
+                    "p (m g t q i) -> p g m q t i", m=CAPS_OUT, g=GROUPS, t=PACK, i=4
+                )
+                dst = w_grouped[:].rearrange(
+                    "p (g m q i t) -> p g m q t i", g=GROUPS, m=CAPS_OUT, i=4, t=PACK
+                )
+                for g in range(GROUPS):
+                    if g < VECTOR_GROUPS:
+                        nc.vector.tensor_copy(out=dst[:, g], in_=src[:, g])
+                    else:
+                        nc.scalar.copy(out=dst[:, g], in_=src[:, g])
+                w_codes = w_mid.tile([P, GROUPS * COLS], U32, align_bytes=64)
+                w_scales = w_mid.tile([P, GROUPS * COLS], U8, align_bytes=64)
+                nc.vector.quantize_mx(
+                    out=w_codes[:].bitcast(FP8X4), scales=w_scales[:], in_=w_grouped[:]
+                )
+                for g in range(GROUPS):
+                    b_cols = slice(g * BATCH, (g + 1) * BATCH)
+                    w_cols = slice(g * COLS, (g + 1) * COLS)
+                    nc.tensor.matmul_mx(
+                        out=acc[:],
+                        lhsT=x_codes[:, n, c, b_cols].bitcast(FP8X4),
+                        lhsT_scale=x_scales[:, n, c, b_cols],
+                        rhs=w_codes[:, w_cols].bitcast(FP8X4),
+                        rhs_scale=w_scales[:, w_cols],
+                        start=(c == 0 and g == 0),
+                        stop=(c == CLASSES - 1 and g == GROUPS - 1),
+                    )
+            votes = results.tile([P, COLS], F32)
+            nc.vector.tensor_copy(out=votes[:], in_=acc[:])
+            nc.sync.dma_start(out=out_dram[:, n, :], in_=votes[:])

@@ -25,6 +25,7 @@ CLASSES = 4
 CHUNKS = D_IN // (CLASSES * HALVES * RUN)
 WORDS_OF_RUN = RUN // 2
 VECTOR_GROUPS = 2
+W_AHEAD = 6
 
 FLOPS = 2 * BATCH * CAPS_IN * D_IN * COLS
 
@@ -39,15 +40,18 @@ def tile_transforming_k_kernel(tc, inputs, transform_mat, out):
     )
     out_dram = out.rearrange("b n m o one -> b n (m o one)")
 
+    units = [(n, c) for n in range(CAPS_IN) for c in range(CLASSES)]
+
     with ExitStack() as ctx:
         keep = ctx.enter_context(tc.tile_pool(name="keep", bufs=1))
-        x_in = ctx.enter_context(tc.tile_pool(name="x_in", bufs=CAPS_IN))
+        x_in = ctx.enter_context(tc.tile_pool(name="x_in", bufs=3))
         x_mid = ctx.enter_context(tc.tile_pool(name="x_mid", bufs=3))
-        w_in = ctx.enter_context(tc.tile_pool(name="w_in", bufs=6))
+        w_in = ctx.enter_context(tc.tile_pool(name="w_in", bufs=W_AHEAD))
         w_mid = ctx.enter_context(tc.tile_pool(name="w_mid", bufs=3))
         results = ctx.enter_context(tc.tile_pool(name="results", bufs=2))
         psum_t = ctx.enter_context(tc.psum_pool(name="psum_t", bufs=4))
         psum_acc = ctx.enter_context(tc.psum_pool(name="psum_acc", bufs=2))
+        ctx.enter_context(tc.manual_schedule())
 
         ident = keep.tile([P, P], F32)
         make_identity(nc, ident[:])
@@ -55,77 +59,119 @@ def tile_transforming_k_kernel(tc, inputs, transform_mat, out):
         x_codes = keep.tile([P, CAPS_IN, CLASSES, GROUPS * BATCH], U32, align_bytes=64)
         x_scales = keep.tile([P, CAPS_IN, CLASSES, GROUPS * BATCH], U8, align_bytes=64)
 
-        for n in range(CAPS_IN):
+        x_rows_of = {}
+        x_grouped_of = {}
+        w_rows_of = {}
+        w_grouped_of = {}
+        acc_of = {}
+
+        def load_x(n):
             x_rows = x_in.tile([P, D_IN], BF16)
             nc.sync.dma_start(out=x_rows[:], in_=x_dram[:, n, :])
-            by_class = x_rows[:].rearrange("b (j c s) -> b c j s", c=CLASSES, s=HALVES * RUN)
-            for c in range(CLASSES):
-                x_sorted = x_mid.tile([P, P * RUN], BF16)
-                nc.vector.tensor_copy(
-                    out=x_sorted[:].rearrange("b (j s) -> b j s", s=HALVES * RUN),
-                    in_=by_class[:, c],
-                )
-                x_words = x_sorted[:].bitcast(F32).rearrange("b (p w) -> b p w", w=WORDS_OF_RUN)
-                x_grouped = x_mid.tile([P, GROUPS * BATCH * PACK], BF16, align_bytes=64)
-                grouped_words = x_grouped[:].bitcast(F32).rearrange(
-                    "p (g b u) -> p g b u", g=GROUPS, b=BATCH
-                )
-                for first_g in range(0, GROUPS, 2):
-                    xt = psum_t.tile([P, 4 * BATCH], F32)
-                    for w in range(4):
-                        nc.tensor.transpose(
-                            xt[:, w * BATCH : (w + 1) * BATCH],
-                            x_words[:, :, 2 * first_g + w],
-                            ident[:],
-                        )
-                    nc.scalar.copy(
-                        out=grouped_words[:, first_g : first_g + 2],
-                        in_=xt[:].rearrange("p (g u b) -> p g b u", g=2, u=2),
-                    )
-                nc.vector.quantize_mx(
-                    out=x_codes[:, n, c, :].bitcast(FP8X4),
-                    scales=x_scales[:, n, c, :],
-                    in_=x_grouped[:],
-                )
+            x_rows_of[n] = x_rows
 
-        for n in range(CAPS_IN):
-            acc = psum_acc.tile([P, COLS], F32)
-            for c in range(CLASSES):
-                w_rows = w_in.tile([P, CAPS_OUT * RUN * D_OUT], BF16)
-                for h in range(HALVES):
-                    nc.sync.dma_start(
-                        out=w_rows[h:P:HALVES, :].rearrange("p (m e) -> p m e", m=CAPS_OUT),
-                        in_=w_dram[n, c, h],
+        def load_w(n, c):
+            if c == 0 and n + 1 < CAPS_IN:
+                load_x(n + 1)
+            w_rows = w_in.tile([P, CAPS_OUT * RUN * D_OUT], BF16)
+            for h in range(HALVES):
+                nc.sync.dma_start(
+                    out=w_rows[h:P:HALVES, :].rearrange("p (m e) -> p m e", m=CAPS_OUT),
+                    in_=w_dram[n, c, h],
+                )
+            w_rows_of[(n, c)] = w_rows
+
+        def transpose_x(n, c):
+            by_class = x_rows_of[n][:].rearrange("b (j c s) -> b c j s", c=CLASSES, s=HALVES * RUN)
+            x_sorted = x_mid.tile([P, P * RUN], BF16)
+            nc.vector.tensor_copy(
+                out=x_sorted[:].rearrange("b (j s) -> b j s", s=HALVES * RUN), in_=by_class[:, c]
+            )
+            x_words = x_sorted[:].bitcast(F32).rearrange("b (p w) -> b p w", w=WORDS_OF_RUN)
+            x_grouped = x_mid.tile([P, GROUPS * BATCH * PACK], BF16, align_bytes=64)
+            grouped_words = x_grouped[:].bitcast(F32).rearrange(
+                "p (g b u) -> p g b u", g=GROUPS, b=BATCH
+            )
+            for first_g in range(0, GROUPS, 2):
+                xt = psum_t.tile([P, 4 * BATCH], F32)
+                for w in range(4):
+                    nc.tensor.transpose(
+                        xt[:, w * BATCH : (w + 1) * BATCH],
+                        x_words[:, :, 2 * first_g + w],
+                        ident[:],
                     )
-                w_grouped = w_mid.tile([P, GROUPS * COLS * PACK], BF16, align_bytes=64)
-                src = w_rows[:].rearrange(
-                    "p (m g t q i) -> p g m q t i", m=CAPS_OUT, g=GROUPS, t=PACK, i=4
+                nc.scalar.copy(
+                    out=grouped_words[:, first_g : first_g + 2],
+                    in_=xt[:].rearrange("p (g u b) -> p g b u", g=2, u=2),
                 )
-                dst = w_grouped[:].rearrange(
-                    "p (g m q i t) -> p g m q t i", g=GROUPS, m=CAPS_OUT, i=4, t=PACK
+            x_grouped_of[(n, c)] = x_grouped
+
+        def quantise_x(n, c):
+            nc.vector.quantize_mx(
+                out=x_codes[:, n, c, :].bitcast(FP8X4),
+                scales=x_scales[:, n, c, :],
+                in_=x_grouped_of[(n, c)][:],
+            )
+
+        def regroup_w(n, c):
+            w_grouped = w_mid.tile([P, GROUPS * COLS * PACK], BF16, align_bytes=64)
+            src = w_rows_of[(n, c)][:].rearrange(
+                "p (m g t q i) -> p g m q t i", m=CAPS_OUT, g=GROUPS, t=PACK, i=4
+            )
+            dst = w_grouped[:].rearrange(
+                "p (g m q i t) -> p g m q t i", g=GROUPS, m=CAPS_OUT, i=4, t=PACK
+            )
+            for g in range(GROUPS):
+                if g < VECTOR_GROUPS:
+                    nc.vector.tensor_copy(out=dst[:, g], in_=src[:, g])
+                else:
+                    nc.scalar.copy(out=dst[:, g], in_=src[:, g])
+            w_grouped_of[(n, c)] = w_grouped
+
+        def multiply(n, c):
+            w_codes = w_mid.tile([P, GROUPS * COLS], U32, align_bytes=64)
+            w_scales = w_mid.tile([P, GROUPS * COLS], U8, align_bytes=64)
+            nc.vector.quantize_mx(
+                out=w_codes[:].bitcast(FP8X4), scales=w_scales[:], in_=w_grouped_of[(n, c)][:]
+            )
+            if c == 0:
+                acc = psum_acc.tile([P, COLS], F32)
+                acc_of[n] = acc
+            for g in range(GROUPS):
+                b_cols = slice(g * BATCH, (g + 1) * BATCH)
+                w_cols = slice(g * COLS, (g + 1) * COLS)
+                nc.tensor.matmul_mx(
+                    out=acc_of[n][:],
+                    lhsT=x_codes[:, n, c, b_cols].bitcast(FP8X4),
+                    lhsT_scale=x_scales[:, n, c, b_cols],
+                    rhs=w_codes[:, w_cols].bitcast(FP8X4),
+                    rhs_scale=w_scales[:, w_cols],
+                    start=(c == 0 and g == 0),
+                    stop=(c == CLASSES - 1 and g == GROUPS - 1),
                 )
-                for g in range(GROUPS):
-                    if g < VECTOR_GROUPS:
-                        nc.vector.tensor_copy(out=dst[:, g], in_=src[:, g])
-                    else:
-                        nc.scalar.copy(out=dst[:, g], in_=src[:, g])
-                w_codes = w_mid.tile([P, GROUPS * COLS], U32, align_bytes=64)
-                w_scales = w_mid.tile([P, GROUPS * COLS], U8, align_bytes=64)
-                nc.vector.quantize_mx(
-                    out=w_codes[:].bitcast(FP8X4), scales=w_scales[:], in_=w_grouped[:]
-                )
-                for g in range(GROUPS):
-                    b_cols = slice(g * BATCH, (g + 1) * BATCH)
-                    w_cols = slice(g * COLS, (g + 1) * COLS)
-                    nc.tensor.matmul_mx(
-                        out=acc[:],
-                        lhsT=x_codes[:, n, c, b_cols].bitcast(FP8X4),
-                        lhsT_scale=x_scales[:, n, c, b_cols],
-                        rhs=w_codes[:, w_cols].bitcast(FP8X4),
-                        rhs_scale=w_scales[:, w_cols],
-                        start=(c == 0 and g == 0),
-                        stop=(c == CLASSES - 1 and g == GROUPS - 1),
-                    )
-            votes = results.tile([P, COLS], F32)
-            nc.vector.tensor_copy(out=votes[:], in_=acc[:])
-            nc.sync.dma_start(out=out_dram[:, n, :], in_=votes[:])
+            if c == CLASSES - 1:
+                votes = results.tile([P, COLS], F32)
+                nc.vector.tensor_copy(out=votes[:], in_=acc_of[n][:])
+                nc.sync.dma_start(out=out_dram[:, n, :], in_=votes[:])
+
+        load_x(0)
+        for n, c in units[:W_AHEAD]:
+            load_w(n, c)
+        for c in range(CLASSES):
+            transpose_x(0, c)
+            if c > 0:
+                quantise_x(0, c - 1)
+        x_waiting = (0, CLASSES - 1)
+
+        for u, (n, c) in enumerate(units):
+            regroup_w(n, c)
+            if u + W_AHEAD < len(units):
+                load_w(*units[u + W_AHEAD])
+            if n + 1 < CAPS_IN:
+                transpose_x(n + 1, c)
+            if u > 0:
+                multiply(*units[u - 1])
+            if x_waiting is not None:
+                quantise_x(*x_waiting)
+            x_waiting = (n + 1, c) if n + 1 < CAPS_IN else None
+        multiply(*units[-1])

@@ -25,7 +25,8 @@ CLASSES = 4
 CHUNKS = D_IN // (CLASSES * HALVES * RUN)
 WORDS_OF_RUN = RUN // 2
 VECTOR_GROUPS = 2
-W_AHEAD = 6
+PIECES = CLASSES * HALVES
+PIECE = RUN * D_OUT
 
 FLOPS = 2 * BATCH * CAPS_IN * D_IN * COLS
 
@@ -35,9 +36,7 @@ def tile_transforming_k_kernel(tc, inputs, transform_mat, out):
     assert CHUNKS * HALVES == P
 
     x_dram = inputs.rearrange("b n i one -> b n (i one)")
-    w_dram = transform_mat.rearrange(
-        "one n m (j c h r) o uno -> (one n) c h j m (r o uno)", j=CHUNKS, c=CLASSES, h=HALVES, r=RUN
-    )
+    w_dram = transform_mat.rearrange("one n m (j r) o uno -> (one n) j m (r o uno)", j=CHUNKS)
     out_dram = out.rearrange("b n m o one -> b n (m o one)")
 
     units = [(n, c) for n in range(CAPS_IN) for c in range(CLASSES)]
@@ -46,7 +45,7 @@ def tile_transforming_k_kernel(tc, inputs, transform_mat, out):
         keep = ctx.enter_context(tc.tile_pool(name="keep", bufs=1))
         x_in = ctx.enter_context(tc.tile_pool(name="x_in", bufs=3))
         x_mid = ctx.enter_context(tc.tile_pool(name="x_mid", bufs=3))
-        w_in = ctx.enter_context(tc.tile_pool(name="w_in", bufs=W_AHEAD))
+        w_in = ctx.enter_context(tc.tile_pool(name="w_in", bufs=2))
         w_mid = ctx.enter_context(tc.tile_pool(name="w_mid", bufs=3))
         results = ctx.enter_context(tc.tile_pool(name="results", bufs=2))
         psum_t = ctx.enter_context(tc.psum_pool(name="psum_t", bufs=4))
@@ -70,23 +69,28 @@ def tile_transforming_k_kernel(tc, inputs, transform_mat, out):
             nc.sync.dma_start(out=x_rows[:], in_=x_dram[:, n, :])
             x_rows_of[n] = x_rows
 
-        def load_w(n, c):
-            if c == 0 and n + 1 < CAPS_IN:
-                load_x(n + 1)
-            w_rows = w_in.tile([P, CAPS_OUT * RUN * D_OUT], BF16)
-            for h in range(HALVES):
+        def load_w(n):
+            w_rows = w_in.tile([P, CAPS_OUT * CLASSES * PIECE], BF16)
+            for cut in range(CLASSES + 1):
+                first = max(2 * cut - 1, 0)
+                last = min(2 * cut + 1, PIECES)
+                slot = first // HALVES
                 nc.sync.dma_start(
-                    out=w_rows[h:P:HALVES, :].rearrange("p (m e) -> p m e", m=CAPS_OUT),
-                    in_=w_dram[n, c, h],
+                    out=w_rows[cut % 2 : P : 2, :].rearrange("p (m e) -> p m e", m=CAPS_OUT)[
+                        :, :, slot * PIECE : (slot + last - first) * PIECE
+                    ],
+                    in_=w_dram[n, :, :, first * PIECE : last * PIECE],
                 )
-            w_rows_of[(n, c)] = w_rows
+            w_rows_of[n] = w_rows
 
         def transpose_x(n, c):
-            by_class = x_rows_of[n][:].rearrange("b (j c s) -> b c j s", c=CLASSES, s=HALVES * RUN)
-            x_sorted = x_mid.tile([P, P * RUN], BF16)
-            nc.vector.tensor_copy(
-                out=x_sorted[:].rearrange("b (j s) -> b j s", s=HALVES * RUN), in_=by_class[:, c]
+            by_class = x_rows_of[n][:].rearrange(
+                "b (j c h r) -> b c h j r", c=CLASSES, h=HALVES, r=RUN
             )
+            x_sorted = x_mid.tile([P, P * RUN], BF16)
+            by_parity = x_sorted[:].rearrange("b (j z r) -> b z j r", z=HALVES, r=RUN)
+            for h in range(HALVES):
+                nc.vector.tensor_copy(out=by_parity[:, (h + c) % 2], in_=by_class[:, c, h])
             x_words = x_sorted[:].bitcast(F32).rearrange("b (p w) -> b p w", w=WORDS_OF_RUN)
             x_grouped = x_mid.tile([P, GROUPS * BATCH * PACK], BF16, align_bytes=64)
             grouped_words = x_grouped[:].bitcast(F32).rearrange(
@@ -115,9 +119,9 @@ def tile_transforming_k_kernel(tc, inputs, transform_mat, out):
 
         def regroup_w(n, c):
             w_grouped = w_mid.tile([P, GROUPS * COLS * PACK], BF16, align_bytes=64)
-            src = w_rows_of[(n, c)][:].rearrange(
-                "p (m g t q i) -> p g m q t i", m=CAPS_OUT, g=GROUPS, t=PACK, i=4
-            )
+            src = w_rows_of[n][:].rearrange(
+                "p (m c g t q i) -> p c g m q t i", m=CAPS_OUT, c=CLASSES, g=GROUPS, t=PACK, i=4
+            )[:, c]
             dst = w_grouped[:].rearrange(
                 "p (g m q i t) -> p g m q t i", g=GROUPS, m=CAPS_OUT, i=4, t=PACK
             )
@@ -151,12 +155,12 @@ def tile_transforming_k_kernel(tc, inputs, transform_mat, out):
                 )
             if c == CLASSES - 1:
                 votes = results.tile([P, COLS], F32)
-                nc.vector.tensor_copy(out=votes[:], in_=acc_of[n][:])
+                nc.scalar.copy(out=votes[:], in_=acc_of[n][:])
                 nc.sync.dma_start(out=out_dram[:, n, :], in_=votes[:])
 
         load_x(0)
-        for n, c in units[:W_AHEAD]:
-            load_w(n, c)
+        load_x(1)
+        load_w(0)
         for c in range(CLASSES):
             transpose_x(0, c)
             if c > 0:
@@ -164,9 +168,11 @@ def tile_transforming_k_kernel(tc, inputs, transform_mat, out):
         x_waiting = (0, CLASSES - 1)
 
         for u, (n, c) in enumerate(units):
+            if c == 0 and n + 2 < CAPS_IN:
+                load_x(n + 2)
+            if c == 0 and n + 1 < CAPS_IN:
+                load_w(n + 1)
             regroup_w(n, c)
-            if u + W_AHEAD < len(units):
-                load_w(*units[u + W_AHEAD])
             if n + 1 < CAPS_IN:
                 transpose_x(n + 1, c)
             if u > 0:

@@ -25,8 +25,8 @@ CLASSES = 4
 CHUNKS = D_IN // (CLASSES * HALVES * RUN)
 WORDS_OF_RUN = RUN // 2
 VECTOR_GROUPS = 2
-PIECES = CLASSES * HALVES
-PIECE = RUN * D_OUT
+W_AHEAD = 6
+X_AHEAD = 2
 
 FLOPS = 2 * BATCH * CAPS_IN * D_IN * COLS
 
@@ -36,7 +36,9 @@ def tile_transforming_k_kernel(tc, inputs, transform_mat, out):
     assert CHUNKS * HALVES == P
 
     x_dram = inputs.rearrange("b n i one -> b n (i one)")
-    w_dram = transform_mat.rearrange("one n m (j r) o uno -> (one n) j m (r o uno)", j=CHUNKS)
+    w_dram = transform_mat.rearrange(
+        "one n m (j c h r) o uno -> (one n) c h j m (r o uno)", j=CHUNKS, c=CLASSES, h=HALVES, r=RUN
+    )
     out_dram = out.rearrange("b n m o one -> b n (m o one)")
 
     units = [(n, c) for n in range(CAPS_IN) for c in range(CLASSES)]
@@ -45,7 +47,7 @@ def tile_transforming_k_kernel(tc, inputs, transform_mat, out):
         keep = ctx.enter_context(tc.tile_pool(name="keep", bufs=1))
         x_in = ctx.enter_context(tc.tile_pool(name="x_in", bufs=3))
         x_mid = ctx.enter_context(tc.tile_pool(name="x_mid", bufs=3))
-        w_in = ctx.enter_context(tc.tile_pool(name="w_in", bufs=2))
+        w_in = ctx.enter_context(tc.tile_pool(name="w_in", bufs=W_AHEAD))
         w_mid = ctx.enter_context(tc.tile_pool(name="w_mid", bufs=3))
         results = ctx.enter_context(tc.tile_pool(name="results", bufs=2))
         psum_t = ctx.enter_context(tc.psum_pool(name="psum_t", bufs=4))
@@ -69,28 +71,23 @@ def tile_transforming_k_kernel(tc, inputs, transform_mat, out):
             nc.sync.dma_start(out=x_rows[:], in_=x_dram[:, n, :])
             x_rows_of[n] = x_rows
 
-        def load_w(n):
-            w_rows = w_in.tile([P, CAPS_OUT * CLASSES * PIECE], BF16)
-            for cut in range(CLASSES + 1):
-                first = max(2 * cut - 1, 0)
-                last = min(2 * cut + 1, PIECES)
-                slot = first // HALVES
+        def load_w(n, c):
+            if c == CLASSES - X_AHEAD and n + 1 < CAPS_IN:
+                load_x(n + 1)
+            w_rows = w_in.tile([P, CAPS_OUT * RUN * D_OUT], BF16)
+            for h in range(HALVES):
                 nc.sync.dma_start(
-                    out=w_rows[cut % 2 : P : 2, :].rearrange("p (m e) -> p m e", m=CAPS_OUT)[
-                        :, :, slot * PIECE : (slot + last - first) * PIECE
-                    ],
-                    in_=w_dram[n, :, :, first * PIECE : last * PIECE],
+                    out=w_rows[h:P:HALVES, :].rearrange("p (m e) -> p m e", m=CAPS_OUT),
+                    in_=w_dram[n, c, h],
                 )
-            w_rows_of[n] = w_rows
+            w_rows_of[(n, c)] = w_rows
 
         def transpose_x(n, c):
-            by_class = x_rows_of[n][:].rearrange(
-                "b (j c h r) -> b c h j r", c=CLASSES, h=HALVES, r=RUN
-            )
+            by_class = x_rows_of[n][:].rearrange("b (j c s) -> b c j s", c=CLASSES, s=HALVES * RUN)
             x_sorted = x_mid.tile([P, P * RUN], BF16)
-            by_parity = x_sorted[:].rearrange("b (j z r) -> b z j r", z=HALVES, r=RUN)
-            for h in range(HALVES):
-                nc.vector.tensor_copy(out=by_parity[:, (h + c) % 2], in_=by_class[:, c, h])
+            nc.vector.tensor_copy(
+                out=x_sorted[:].rearrange("b (j s) -> b j s", s=HALVES * RUN), in_=by_class[:, c]
+            )
             x_words = x_sorted[:].bitcast(F32).rearrange("b (p w) -> b p w", w=WORDS_OF_RUN)
             x_grouped = x_mid.tile([P, GROUPS * BATCH * PACK], BF16, align_bytes=64)
             grouped_words = x_grouped[:].bitcast(F32).rearrange(
@@ -119,9 +116,9 @@ def tile_transforming_k_kernel(tc, inputs, transform_mat, out):
 
         def regroup_w(n, c):
             w_grouped = w_mid.tile([P, GROUPS * COLS * PACK], BF16, align_bytes=64)
-            src = w_rows_of[n][:].rearrange(
-                "p (m c g t q i) -> p c g m q t i", m=CAPS_OUT, c=CLASSES, g=GROUPS, t=PACK, i=4
-            )[:, c]
+            src = w_rows_of[(n, c)][:].rearrange(
+                "p (m g t q i) -> p g m q t i", m=CAPS_OUT, g=GROUPS, t=PACK, i=4
+            )
             dst = w_grouped[:].rearrange(
                 "p (g m q i t) -> p g m q t i", g=GROUPS, m=CAPS_OUT, i=4, t=PACK
             )
@@ -135,9 +132,13 @@ def tile_transforming_k_kernel(tc, inputs, transform_mat, out):
         def multiply(n, c):
             w_codes = w_mid.tile([P, GROUPS * COLS], U32, align_bytes=64)
             w_scales = w_mid.tile([P, GROUPS * COLS], U8, align_bytes=64)
-            nc.vector.quantize_mx(
-                out=w_codes[:].bitcast(FP8X4), scales=w_scales[:], in_=w_grouped_of[(n, c)][:]
-            )
+            for first_g, last_g in ((0, VECTOR_GROUPS), (VECTOR_GROUPS, GROUPS)):
+                share = slice(first_g * COLS, last_g * COLS)
+                nc.vector.quantize_mx(
+                    out=w_codes[:, share].bitcast(FP8X4),
+                    scales=w_scales[:, share],
+                    in_=w_grouped_of[(n, c)][:, first_g * COLS * PACK : last_g * COLS * PACK],
+                )
             if c == 0:
                 acc = psum_acc.tile([P, COLS], F32)
                 acc_of[n] = acc
@@ -153,31 +154,34 @@ def tile_transforming_k_kernel(tc, inputs, transform_mat, out):
                     start=(c == 0 and g == 0),
                     stop=(c == CLASSES - 1 and g == GROUPS - 1),
                 )
-            if c == CLASSES - 1:
-                votes = results.tile([P, COLS], F32)
-                nc.scalar.copy(out=votes[:], in_=acc_of[n][:])
-                nc.sync.dma_start(out=out_dram[:, n, :], in_=votes[:])
+
+        def store(n):
+            votes = results.tile([P, COLS], F32)
+            nc.scalar.copy(out=votes[:], in_=acc_of[n][:])
+            nc.sync.dma_start(out=out_dram[:, n, :], in_=votes[:])
 
         load_x(0)
-        load_x(1)
-        load_w(0)
-        for c in range(CLASSES):
-            transpose_x(0, c)
-            if c > 0:
-                quantise_x(0, c - 1)
-        x_waiting = (0, CLASSES - 1)
+        for n, c in units[:W_AHEAD]:
+            load_w(n, c)
+        x_waiting = None
+        for n, c in units[:X_AHEAD]:
+            transpose_x(n, c)
+            if x_waiting is not None:
+                quantise_x(*x_waiting)
+            x_waiting = (n, c)
 
         for u, (n, c) in enumerate(units):
-            if c == 0 and n + 2 < CAPS_IN:
-                load_x(n + 2)
-            if c == 0 and n + 1 < CAPS_IN:
-                load_w(n + 1)
             regroup_w(n, c)
-            if n + 1 < CAPS_IN:
-                transpose_x(n + 1, c)
+            if u + W_AHEAD < len(units):
+                load_w(*units[u + W_AHEAD])
+            if u + X_AHEAD < len(units):
+                transpose_x(*units[u + X_AHEAD])
             if u > 0:
                 multiply(*units[u - 1])
             if x_waiting is not None:
                 quantise_x(*x_waiting)
-            x_waiting = (n + 1, c) if n + 1 < CAPS_IN else None
+            x_waiting = units[u + X_AHEAD] if u + X_AHEAD < len(units) else None
+            if c == 1 and n > 0:
+                store(n - 1)
         multiply(*units[-1])
+        store(CAPS_IN - 1)

@@ -25,7 +25,7 @@ CLASSES = 4
 CHUNKS = D_IN // (CLASSES * HALVES * RUN)
 WORDS_OF_RUN = RUN // 2
 VECTOR_GROUPS = 2
-W_AHEAD = 6
+W_AHEAD = 8
 X_AHEAD = 2
 
 FLOPS = 2 * BATCH * CAPS_IN * D_IN * COLS
@@ -82,17 +82,20 @@ def tile_transforming_k_kernel(tc, inputs, transform_mat, out):
                 )
             w_rows_of[(n, c)] = w_rows
 
-        def transpose_x(n, c):
+        x_sorted_of = {}
+        x_banks_of = {}
+
+        def sort_x(n, c):
             by_class = x_rows_of[n][:].rearrange("b (j c s) -> b c j s", c=CLASSES, s=HALVES * RUN)
             x_sorted = x_mid.tile([P, P * RUN], BF16)
             nc.vector.tensor_copy(
                 out=x_sorted[:].rearrange("b (j s) -> b j s", s=HALVES * RUN), in_=by_class[:, c]
             )
-            x_words = x_sorted[:].bitcast(F32).rearrange("b (p w) -> b p w", w=WORDS_OF_RUN)
-            x_grouped = x_mid.tile([P, GROUPS * BATCH * PACK], BF16, align_bytes=64)
-            grouped_words = x_grouped[:].bitcast(F32).rearrange(
-                "p (g b u) -> p g b u", g=GROUPS, b=BATCH
-            )
+            x_sorted_of[(n, c)] = x_sorted
+
+        def turn_x(n, c):
+            x_words = x_sorted_of[(n, c)][:].bitcast(F32).rearrange("b (p w) -> b p w", w=WORDS_OF_RUN)
+            banks = []
             for first_g in range(0, GROUPS, 2):
                 xt = psum_t.tile([P, 4 * BATCH], F32)
                 for w in range(4):
@@ -101,8 +104,17 @@ def tile_transforming_k_kernel(tc, inputs, transform_mat, out):
                         x_words[:, :, 2 * first_g + w],
                         ident[:],
                     )
+                banks.append(xt)
+            x_banks_of[(n, c)] = banks
+
+        def copy_x(n, c):
+            x_grouped = x_mid.tile([P, GROUPS * BATCH * PACK], BF16, align_bytes=64)
+            grouped_words = x_grouped[:].bitcast(F32).rearrange(
+                "p (g b u) -> p g b u", g=GROUPS, b=BATCH
+            )
+            for i, xt in enumerate(x_banks_of[(n, c)]):
                 nc.scalar.copy(
-                    out=grouped_words[:, first_g : first_g + 2],
+                    out=grouped_words[:, 2 * i : 2 * i + 2],
                     in_=xt[:].rearrange("p (g u b) -> p g b u", g=2, u=2),
                 )
             x_grouped_of[(n, c)] = x_grouped
@@ -163,24 +175,26 @@ def tile_transforming_k_kernel(tc, inputs, transform_mat, out):
         load_x(0)
         for n, c in units[:W_AHEAD]:
             load_w(n, c)
-        x_waiting = None
-        for n, c in units[:X_AHEAD]:
-            transpose_x(n, c)
-            if x_waiting is not None:
-                quantise_x(*x_waiting)
-            x_waiting = (n, c)
+        sort_x(*units[0])
+        turn_x(*units[0])
+        copy_x(*units[0])
+        sort_x(*units[1])
+        turn_x(*units[1])
+        quantise_x(*units[0])
 
         for u, (n, c) in enumerate(units):
+            if u + X_AHEAD < len(units):
+                sort_x(*units[u + X_AHEAD])
+                turn_x(*units[u + X_AHEAD])
+            if u + 1 < len(units):
+                copy_x(*units[u + 1])
             regroup_w(n, c)
             if u + W_AHEAD < len(units):
                 load_w(*units[u + W_AHEAD])
-            if u + X_AHEAD < len(units):
-                transpose_x(*units[u + X_AHEAD])
             if u > 0:
                 multiply(*units[u - 1])
-            if x_waiting is not None:
-                quantise_x(*x_waiting)
-            x_waiting = units[u + X_AHEAD] if u + X_AHEAD < len(units) else None
+            if u + 1 < len(units):
+                quantise_x(*units[u + 1])
             if c == 1 and n > 0:
                 store(n - 1)
         multiply(*units[-1])

@@ -25,8 +25,8 @@ CLASSES = 4
 CHUNKS = D_IN // (CLASSES * HALVES * RUN)
 WORDS_OF_RUN = RUN // 2
 VECTOR_GROUPS = 2
-W_AHEAD = 8
-X_AHEAD = 2
+LAST_VECTOR_GROUPS = 3
+RUN_ELEMS = RUN * D_OUT
 
 FLOPS = 2 * BATCH * CAPS_IN * D_IN * COLS
 
@@ -36,9 +36,7 @@ def tile_transforming_k_kernel(tc, inputs, transform_mat, out):
     assert CHUNKS * HALVES == P
 
     x_dram = inputs.rearrange("b n i one -> b n (i one)")
-    w_dram = transform_mat.rearrange(
-        "one n m (j c h r) o uno -> (one n) c h j m (r o uno)", j=CHUNKS, c=CLASSES, h=HALVES, r=RUN
-    )
+    w_dram = transform_mat.rearrange("one n m (j s) o uno -> (one n) j m (s o uno)", j=CHUNKS)
     out_dram = out.rearrange("b n m o one -> b n (m o one)")
 
     units = [(n, c) for n in range(CAPS_IN) for c in range(CLASSES)]
@@ -47,7 +45,8 @@ def tile_transforming_k_kernel(tc, inputs, transform_mat, out):
         keep = ctx.enter_context(tc.tile_pool(name="keep", bufs=1))
         x_in = ctx.enter_context(tc.tile_pool(name="x_in", bufs=3))
         x_mid = ctx.enter_context(tc.tile_pool(name="x_mid", bufs=3))
-        w_in = ctx.enter_context(tc.tile_pool(name="w_in", bufs=W_AHEAD))
+        w_pairs = ctx.enter_context(tc.tile_pool(name="w_pairs", bufs=4))
+        w_singles = ctx.enter_context(tc.tile_pool(name="w_singles", bufs=2))
         w_mid = ctx.enter_context(tc.tile_pool(name="w_mid", bufs=3))
         results = ctx.enter_context(tc.tile_pool(name="results", bufs=2))
         psum_t = ctx.enter_context(tc.psum_pool(name="psum_t", bufs=4))
@@ -64,6 +63,7 @@ def tile_transforming_k_kernel(tc, inputs, transform_mat, out):
         x_grouped_of = {}
         w_rows_of = {}
         w_grouped_of = {}
+        w_mx_of = {}
         acc_of = {}
 
         def load_x(n):
@@ -71,25 +71,40 @@ def tile_transforming_k_kernel(tc, inputs, transform_mat, out):
             nc.sync.dma_start(out=x_rows[:], in_=x_dram[:, n, :])
             x_rows_of[n] = x_rows
 
-        def load_w(n, c):
-            if c == CLASSES - X_AHEAD and n + 1 < CAPS_IN:
-                load_x(n + 1)
-            w_rows = w_in.tile([P, CAPS_OUT * RUN * D_OUT], BF16)
-            for h in range(HALVES):
-                nc.sync.dma_start(
-                    out=w_rows[h:P:HALVES, :].rearrange("p (m e) -> p m e", m=CAPS_OUT),
-                    in_=w_dram[n, c, h],
-                )
-            w_rows_of[(n, c)] = w_rows
+        def load_runs(n, parity, run, runs, out):
+            nc.sync.dma_start(
+                out=out[parity:P:HALVES],
+                in_=w_dram[n, :, :, run * RUN_ELEMS : (run + runs) * RUN_ELEMS],
+            )
+
+        def load_single(n, c):
+            w_rows = w_singles.tile([P, CAPS_OUT * RUN_ELEMS], BF16)
+            by_m = w_rows[:].rearrange("p (m e) -> p m e", m=CAPS_OUT)
+            for parity in range(HALVES):
+                load_runs(n, parity, 2 * c + (c + parity) % 2, 1, by_m)
+            w_rows_of[(n, c)] = by_m
+
+        def load_pair(n, c):
+            w_rows = w_pairs.tile([P, CAPS_OUT * 2 * RUN_ELEMS], BF16)
+            by_m = w_rows[:].rearrange("p (m e) -> p m e", m=CAPS_OUT)
+            load_runs(n, 0, 2 * c, 1, by_m[:, :, :RUN_ELEMS])
+            load_runs(n, 1, 2 * c + 1, 2, by_m)
+            load_runs(n, 0, 2 * c + 3, 1, by_m[:, :, RUN_ELEMS:])
+            w_rows_of[(n, c)] = by_m[:, :, :RUN_ELEMS]
+            w_rows_of[(n, c + 1)] = by_m[:, :, RUN_ELEMS:]
 
         x_sorted_of = {}
         x_banks_of = {}
 
         def sort_x(n, c):
-            by_class = x_rows_of[n][:].rearrange("b (j c s) -> b c j s", c=CLASSES, s=HALVES * RUN)
+            by_class = x_rows_of[n][:].rearrange(
+                "b (j c h s) -> b c j h s", c=CLASSES, h=HALVES, s=RUN
+            )[:, c]
+            if c % 2 == 1:
+                by_class = by_class[:, :, ::-1, :]
             x_sorted = x_mid.tile([P, P * RUN], BF16)
             nc.vector.tensor_copy(
-                out=x_sorted[:].rearrange("b (j s) -> b j s", s=HALVES * RUN), in_=by_class[:, c]
+                out=x_sorted[:].rearrange("b (j h s) -> b j h s", h=HALVES, s=RUN), in_=by_class
             )
             x_sorted_of[(n, c)] = x_sorted
 
@@ -126,31 +141,34 @@ def tile_transforming_k_kernel(tc, inputs, transform_mat, out):
                 in_=x_grouped_of[(n, c)][:],
             )
 
-        def regroup_w(n, c):
+        def regroup_w(n, c, vector_groups):
             w_grouped = w_mid.tile([P, GROUPS * COLS * PACK], BF16, align_bytes=64)
-            src = w_rows_of[(n, c)][:].rearrange(
-                "p (m g t q i) -> p g m q t i", m=CAPS_OUT, g=GROUPS, t=PACK, i=4
-            )
+            src = w_rows_of[(n, c)].rearrange("p m (g t q i) -> p g m q t i", g=GROUPS, t=PACK, i=4)
             dst = w_grouped[:].rearrange(
                 "p (g m q i t) -> p g m q t i", g=GROUPS, m=CAPS_OUT, i=4, t=PACK
             )
             for g in range(GROUPS):
-                if g < VECTOR_GROUPS:
+                if g < vector_groups:
                     nc.vector.tensor_copy(out=dst[:, g], in_=src[:, g])
                 else:
                     nc.scalar.copy(out=dst[:, g], in_=src[:, g])
             w_grouped_of[(n, c)] = w_grouped
 
-        def multiply(n, c):
+        def quantise_w(n, c, calls):
             w_codes = w_mid.tile([P, GROUPS * COLS], U32, align_bytes=64)
             w_scales = w_mid.tile([P, GROUPS * COLS], U8, align_bytes=64)
-            for first_g, last_g in ((0, VECTOR_GROUPS), (VECTOR_GROUPS, GROUPS)):
+            w_mx_of[(n, c)] = (w_codes, w_scales)
+            for i in range(calls):
+                first_g, last_g = i * GROUPS // calls, (i + 1) * GROUPS // calls
                 share = slice(first_g * COLS, last_g * COLS)
                 nc.vector.quantize_mx(
                     out=w_codes[:, share].bitcast(FP8X4),
                     scales=w_scales[:, share],
                     in_=w_grouped_of[(n, c)][:, first_g * COLS * PACK : last_g * COLS * PACK],
                 )
+
+        def multiply(n, c):
+            w_codes, w_scales = w_mx_of[(n, c)]
             if c == 0:
                 acc = psum_acc.tile([P, COLS], F32)
                 acc_of[n] = acc
@@ -172,30 +190,43 @@ def tile_transforming_k_kernel(tc, inputs, transform_mat, out):
             nc.scalar.copy(out=votes[:], in_=acc_of[n][:])
             nc.sync.dma_start(out=out_dram[:, n, :], in_=votes[:])
 
+        last = len(units) - 1
+        load_single(0, 0)
         load_x(0)
-        for n, c in units[:W_AHEAD]:
-            load_w(n, c)
-        sort_x(*units[0])
-        turn_x(*units[0])
+        load_single(0, 1)
+        load_pair(0, 2)
+        load_x(1)
+        load_pair(1, 0)
+        load_pair(1, 2)
+        load_x(2)
+        load_pair(2, 0)
+        regroup_w(*units[0], VECTOR_GROUPS)
+        for u in range(2):
+            sort_x(*units[u])
+            turn_x(*units[u])
         copy_x(*units[0])
-        sort_x(*units[1])
-        turn_x(*units[1])
-        quantise_x(*units[0])
 
         for u, (n, c) in enumerate(units):
-            if u + X_AHEAD < len(units):
-                sort_x(*units[u + X_AHEAD])
-                turn_x(*units[u + X_AHEAD])
-            if u + 1 < len(units):
-                copy_x(*units[u + 1])
-            regroup_w(n, c)
-            if u + W_AHEAD < len(units):
-                load_w(*units[u + W_AHEAD])
             if u > 0:
+                regroup_w(n, c, LAST_VECTOR_GROUPS if u == last else VECTOR_GROUPS)
+            if u < last:
+                copy_x(*units[u + 1])
+            quantise_x(n, c)
+            if u > 0:
+                quantise_w(*units[u - 1], 1)
                 multiply(*units[u - 1])
-            if u + 1 < len(units):
-                quantise_x(*units[u + 1])
+            if u + 2 <= last:
+                sort_x(*units[u + 2])
+                turn_x(*units[u + 2])
+            if u == 3:
+                load_pair(2, 2)
+                load_x(3)
+            if u == 5:
+                load_pair(3, 0)
+                load_single(3, 2)
+                load_single(3, 3)
             if c == 1 and n > 0:
                 store(n - 1)
-        multiply(*units[-1])
+        quantise_w(*units[last], 2)
+        multiply(*units[last])
         store(CAPS_IN - 1)

@@ -23,7 +23,6 @@ RUN = GROUPS * PACK
 HALVES = 2
 CLASSES = 4
 CHUNKS = D_IN // (CLASSES * HALVES * RUN)
-WORDS_OF_RUN = RUN // 2
 VECTOR_GROUPS = 2
 LAST_VECTOR_GROUPS = 3
 RUN_ELEMS = RUN * D_OUT
@@ -56,6 +55,9 @@ def tile_transforming_k_kernel(tc, inputs, transform_mat, out):
         ident = keep.tile([P, P], F32)
         make_identity(nc, ident[:])
 
+        first_copy = keep.tile([P, 1], F32)
+        nc.scalar.copy(out=first_copy[:], in_=ident[:, 0:1])
+
         x_codes = keep.tile([P, CAPS_IN, CLASSES, GROUPS * BATCH], U32, align_bytes=64)
         x_scales = keep.tile([P, CAPS_IN, CLASSES, GROUPS * BATCH], U8, align_bytes=64)
 
@@ -71,17 +73,21 @@ def tile_transforming_k_kernel(tc, inputs, transform_mat, out):
             nc.sync.dma_start(out=x_rows[:], in_=x_dram[:, n, :])
             x_rows_of[n] = x_rows
 
-        def load_runs(n, parity, run, runs, out):
+        def m_parts(parts):
+            return [slice(i * CAPS_OUT // parts, (i + 1) * CAPS_OUT // parts) for i in range(parts)]
+
+        def load_runs(n, parity, run, runs, out, ms=slice(0, CAPS_OUT)):
             nc.sync.dma_start(
-                out=out[parity:P:HALVES],
-                in_=w_dram[n, :, :, run * RUN_ELEMS : (run + runs) * RUN_ELEMS],
+                out=out[parity:P:HALVES, ms],
+                in_=w_dram[n, :, ms, run * RUN_ELEMS : (run + runs) * RUN_ELEMS],
             )
 
-        def load_single(n, c):
+        def load_single(n, c, parts=1):
             w_rows = w_singles.tile([P, CAPS_OUT * RUN_ELEMS], BF16)
             by_m = w_rows[:].rearrange("p (m e) -> p m e", m=CAPS_OUT)
-            for parity in range(HALVES):
-                load_runs(n, parity, 2 * c + (c + parity) % 2, 1, by_m)
+            for ms in m_parts(parts):
+                for parity in range(HALVES):
+                    load_runs(n, parity, 2 * c + (c + parity) % 2, 1, by_m, ms)
             w_rows_of[(n, c)] = by_m
 
         def load_pair(n, c):
@@ -98,25 +104,28 @@ def tile_transforming_k_kernel(tc, inputs, transform_mat, out):
 
         def sort_x(n, c):
             by_class = x_rows_of[n][:].rearrange(
-                "b (j c h s) -> b c j h s", c=CLASSES, h=HALVES, s=RUN
+                "b (j c h g t) -> b c g j h t", c=CLASSES, h=HALVES, g=GROUPS, t=PACK
             )[:, c]
             if c % 2 == 1:
-                by_class = by_class[:, :, ::-1, :]
+                by_class = by_class[:, :, :, ::-1, :]
             x_sorted = x_mid.tile([P, P * RUN], BF16)
             nc.vector.tensor_copy(
-                out=x_sorted[:].rearrange("b (j h s) -> b j h s", h=HALVES, s=RUN), in_=by_class
+                out=x_sorted[:].rearrange("b (g j h t) -> b g j h t", g=GROUPS, h=HALVES, t=PACK),
+                in_=by_class,
             )
             x_sorted_of[(n, c)] = x_sorted
 
         def turn_x(n, c):
-            x_words = x_sorted_of[(n, c)][:].bitcast(F32).rearrange("b (p w) -> b p w", w=WORDS_OF_RUN)
+            x_words = x_sorted_of[(n, c)][:].bitcast(F32).rearrange(
+                "b (g p u) -> b g u p", g=GROUPS, u=2
+            )
             banks = []
             for first_g in range(0, GROUPS, 2):
                 xt = psum_t.tile([P, 4 * BATCH], F32)
                 for w in range(4):
                     nc.tensor.transpose(
                         xt[:, w * BATCH : (w + 1) * BATCH],
-                        x_words[:, :, 2 * first_g + w],
+                        x_words[:, first_g + w // 2, w % 2],
                         ident[:],
                     )
                 banks.append(xt)
@@ -141,17 +150,18 @@ def tile_transforming_k_kernel(tc, inputs, transform_mat, out):
                 in_=x_grouped_of[(n, c)][:],
             )
 
-        def regroup_w(n, c, vector_groups):
+        def regroup_w(n, c, vector_groups=VECTOR_GROUPS, parts=1):
             w_grouped = w_mid.tile([P, GROUPS * COLS * PACK], BF16, align_bytes=64)
             src = w_rows_of[(n, c)].rearrange("p m (g t q i) -> p g m q t i", g=GROUPS, t=PACK, i=4)
             dst = w_grouped[:].rearrange(
                 "p (g m q i t) -> p g m q t i", g=GROUPS, m=CAPS_OUT, i=4, t=PACK
             )
-            for g in range(GROUPS):
-                if g < vector_groups:
-                    nc.vector.tensor_copy(out=dst[:, g], in_=src[:, g])
-                else:
-                    nc.scalar.copy(out=dst[:, g], in_=src[:, g])
+            for ms in m_parts(parts):
+                for g in range(GROUPS):
+                    if g < vector_groups:
+                        nc.vector.tensor_copy(out=dst[:, g, ms], in_=src[:, g, ms])
+                    else:
+                        nc.scalar.copy(out=dst[:, g, ms], in_=src[:, g, ms])
             w_grouped_of[(n, c)] = w_grouped
 
         def quantise_w(n, c, calls):
@@ -200,21 +210,26 @@ def tile_transforming_k_kernel(tc, inputs, transform_mat, out):
         load_pair(1, 2)
         load_x(2)
         load_pair(2, 0)
-        regroup_w(*units[0], VECTOR_GROUPS)
-        for u in range(2):
+        regroup_w(*units[0])
+        for u in range(3):
             sort_x(*units[u])
             turn_x(*units[u])
-        copy_x(*units[0])
+            if u > 0:
+                copy_x(*units[u - 1])
 
         for u, (n, c) in enumerate(units):
-            if u > 0:
-                regroup_w(n, c, LAST_VECTOR_GROUPS if u == last else VECTOR_GROUPS)
+            if u == 0:
+                continue
             if u < last:
+                regroup_w(n, c)
                 copy_x(*units[u + 1])
+            else:
+                regroup_w(n, c, LAST_VECTOR_GROUPS, 2)
+            if u == 1:
+                quantise_x(*units[0])
             quantise_x(n, c)
-            if u > 0:
-                quantise_w(*units[u - 1], 1)
-                multiply(*units[u - 1])
+            quantise_w(*units[u - 1], 1)
+            multiply(*units[u - 1])
             if u + 2 <= last:
                 sort_x(*units[u + 2])
                 turn_x(*units[u + 2])
@@ -224,7 +239,7 @@ def tile_transforming_k_kernel(tc, inputs, transform_mat, out):
             if u == 5:
                 load_pair(3, 0)
                 load_single(3, 2)
-                load_single(3, 3)
+                load_single(3, 3, 2)
             if c == 1 and n > 0:
                 store(n - 1)
         quantise_w(*units[last], 2)

@@ -24,7 +24,11 @@ HALVES = 2
 CLASSES = 4
 CHUNKS = D_IN // (CLASSES * HALVES * RUN)
 VECTOR_GROUPS = 2
+SCALAR_HEAVY = ((0, 3), (2, 1))
 LAST_VECTOR_GROUPS = 3
+LAST_PARTS = 2
+PART_COLS = COLS // LAST_PARTS
+BANK = 512
 RUN_ELEMS = RUN * D_OUT
 
 FLOPS = 2 * BATCH * CAPS_IN * D_IN * COLS
@@ -43,13 +47,16 @@ def tile_transforming_k_kernel(tc, inputs, transform_mat, out):
     with ExitStack() as ctx:
         keep = ctx.enter_context(tc.tile_pool(name="keep", bufs=1))
         x_in = ctx.enter_context(tc.tile_pool(name="x_in", bufs=3))
+        x_rough = ctx.enter_context(tc.tile_pool(name="x_rough", bufs=6))
         x_mid = ctx.enter_context(tc.tile_pool(name="x_mid", bufs=3))
+        x_mx = ctx.enter_context(tc.tile_pool(name="x_mx", bufs=2))
         w_pairs = ctx.enter_context(tc.tile_pool(name="w_pairs", bufs=4))
         w_singles = ctx.enter_context(tc.tile_pool(name="w_singles", bufs=2))
         w_mid = ctx.enter_context(tc.tile_pool(name="w_mid", bufs=3))
         results = ctx.enter_context(tc.tile_pool(name="results", bufs=2))
         psum_t = ctx.enter_context(tc.psum_pool(name="psum_t", bufs=4))
         psum_acc = ctx.enter_context(tc.psum_pool(name="psum_acc", bufs=2))
+        psum_last = ctx.enter_context(tc.psum_pool(name="psum_last", bufs=LAST_PARTS))
         ctx.enter_context(tc.manual_schedule())
 
         ident = keep.tile([P, P], F32)
@@ -58,14 +65,13 @@ def tile_transforming_k_kernel(tc, inputs, transform_mat, out):
         first_copy = keep.tile([P, 1], F32)
         nc.scalar.copy(out=first_copy[:], in_=ident[:, 0:1])
 
-        x_codes = keep.tile([P, CAPS_IN, CLASSES, GROUPS * BATCH], U32, align_bytes=64)
-        x_scales = keep.tile([P, CAPS_IN, CLASSES, GROUPS * BATCH], U8, align_bytes=64)
-
+        x_mx_of = {}
         x_rows_of = {}
         x_grouped_of = {}
         w_rows_of = {}
         w_grouped_of = {}
         w_mx_of = {}
+        last_acc_of = {}
         acc_of = {}
 
         def load_x(n):
@@ -108,7 +114,7 @@ def tile_transforming_k_kernel(tc, inputs, transform_mat, out):
             )[:, c]
             if c % 2 == 1:
                 by_class = by_class[:, :, :, ::-1, :]
-            x_sorted = x_mid.tile([P, P * RUN], BF16)
+            x_sorted = x_rough.tile([P, P * RUN], BF16)
             nc.vector.tensor_copy(
                 out=x_sorted[:].rearrange("b (g j h t) -> b g j h t", g=GROUPS, h=HALVES, t=PACK),
                 in_=by_class,
@@ -133,6 +139,7 @@ def tile_transforming_k_kernel(tc, inputs, transform_mat, out):
 
         def copy_x(n, c):
             x_grouped = x_mid.tile([P, GROUPS * BATCH * PACK], BF16, align_bytes=64)
+            x_grouped_of[(n, c)] = x_grouped
             grouped_words = x_grouped[:].bitcast(F32).rearrange(
                 "p (g b u) -> p g b u", g=GROUPS, b=BATCH
             )
@@ -141,63 +148,82 @@ def tile_transforming_k_kernel(tc, inputs, transform_mat, out):
                     out=grouped_words[:, 2 * i : 2 * i + 2],
                     in_=xt[:].rearrange("p (g u b) -> p g b u", g=2, u=2),
                 )
-            x_grouped_of[(n, c)] = x_grouped
 
         def quantise_x(n, c):
+            if c == 0:
+                x_codes = x_mx.tile([P, CLASSES, GROUPS * BATCH], U32, align_bytes=64)
+                x_scales = x_mx.tile([P, CLASSES, GROUPS * BATCH], U8, align_bytes=64)
+                x_mx_of[n] = (x_codes, x_scales)
+            x_codes, x_scales = x_mx_of[n]
             nc.vector.quantize_mx(
-                out=x_codes[:, n, c, :].bitcast(FP8X4),
-                scales=x_scales[:, n, c, :],
-                in_=x_grouped_of[(n, c)][:],
+                out=x_codes[:, c].bitcast(FP8X4), scales=x_scales[:, c], in_=x_grouped_of[(n, c)][:]
             )
 
-        def regroup_w(n, c, vector_groups=VECTOR_GROUPS, parts=1):
+        def regroup_runs(n, c, ms, out, vector_groups):
+            src = w_rows_of[(n, c)][:, ms].rearrange("p m (g t q i) -> p g m q t i", g=GROUPS, t=PACK, i=4)
+            dst = out.rearrange("p (g m q i t) -> p g m q t i", g=GROUPS, q=D_OUT // 4, i=4, t=PACK)
+            for g in range(GROUPS):
+                if g < vector_groups:
+                    nc.vector.tensor_copy(out=dst[:, g], in_=src[:, g])
+                else:
+                    nc.scalar.copy(out=dst[:, g], in_=src[:, g])
+
+        def quantise_columns(key, first, columns):
+            w_codes, w_scales = w_mx_of[key]
+            share = slice(first, first + columns)
+            nc.vector.quantize_mx(
+                out=w_codes[:, share].bitcast(FP8X4),
+                scales=w_scales[:, share],
+                in_=w_grouped_of[key][:, first * PACK : (first + columns) * PACK],
+            )
+
+        def weight_tiles(key):
             w_grouped = w_mid.tile([P, GROUPS * COLS * PACK], BF16, align_bytes=64)
-            src = w_rows_of[(n, c)].rearrange("p m (g t q i) -> p g m q t i", g=GROUPS, t=PACK, i=4)
-            dst = w_grouped[:].rearrange(
-                "p (g m q i t) -> p g m q t i", g=GROUPS, m=CAPS_OUT, i=4, t=PACK
-            )
-            for ms in m_parts(parts):
-                for g in range(GROUPS):
-                    if g < vector_groups:
-                        nc.vector.tensor_copy(out=dst[:, g, ms], in_=src[:, g, ms])
-                    else:
-                        nc.scalar.copy(out=dst[:, g, ms], in_=src[:, g, ms])
-            w_grouped_of[(n, c)] = w_grouped
-
-        def quantise_w(n, c, calls):
             w_codes = w_mid.tile([P, GROUPS * COLS], U32, align_bytes=64)
             w_scales = w_mid.tile([P, GROUPS * COLS], U8, align_bytes=64)
-            w_mx_of[(n, c)] = (w_codes, w_scales)
-            for i in range(calls):
-                first_g, last_g = i * GROUPS // calls, (i + 1) * GROUPS // calls
-                share = slice(first_g * COLS, last_g * COLS)
-                nc.vector.quantize_mx(
-                    out=w_codes[:, share].bitcast(FP8X4),
-                    scales=w_scales[:, share],
-                    in_=w_grouped_of[(n, c)][:, first_g * COLS * PACK : last_g * COLS * PACK],
-                )
+            w_grouped_of[key] = w_grouped
+            w_mx_of[key] = (w_codes, w_scales)
 
-        def multiply(n, c):
+        def regroup_w(n, c):
+            weight_tiles((n, c))
+            vector_groups = 1 if (n, c) in SCALAR_HEAVY else VECTOR_GROUPS
+            regroup_runs(n, c, slice(0, CAPS_OUT), w_grouped_of[(n, c)][:], vector_groups)
+
+        def quantise_w(n, c):
+            quantise_columns((n, c), 0, GROUPS * COLS)
+
+        def multiply_columns(n, c, acc, first, step, columns):
             w_codes, w_scales = w_mx_of[(n, c)]
-            if c == 0:
-                acc = psum_acc.tile([P, COLS], F32)
-                acc_of[n] = acc
+            x_codes, x_scales = x_mx_of[n]
             for g in range(GROUPS):
                 b_cols = slice(g * BATCH, (g + 1) * BATCH)
-                w_cols = slice(g * COLS, (g + 1) * COLS)
+                w_cols = slice(first + g * step, first + g * step + columns)
                 nc.tensor.matmul_mx(
-                    out=acc_of[n][:],
-                    lhsT=x_codes[:, n, c, b_cols].bitcast(FP8X4),
-                    lhsT_scale=x_scales[:, n, c, b_cols],
+                    out=acc[:, 0:columns],
+                    lhsT=x_codes[:, c, b_cols].bitcast(FP8X4),
+                    lhsT_scale=x_scales[:, c, b_cols],
                     rhs=w_codes[:, w_cols].bitcast(FP8X4),
                     rhs_scale=w_scales[:, w_cols],
                     start=(c == 0 and g == 0),
                     stop=(c == CLASSES - 1 and g == GROUPS - 1),
                 )
 
+        def multiply(n, c):
+            if n < CAPS_IN - 1:
+                if c == 0:
+                    acc = psum_acc.tile([P, BANK], F32)
+                    acc_of[n] = acc
+                multiply_columns(n, c, acc_of[n], 0, COLS, COLS)
+            else:
+                for part in range(LAST_PARTS):
+                    if c == 0:
+                        last_acc = psum_last.tile([P, BANK], F32)
+                        last_acc_of[part] = last_acc
+                    multiply_columns(n, c, last_acc_of[part], part * PART_COLS, COLS, PART_COLS)
+
         def store(n):
             votes = results.tile([P, COLS], F32)
-            nc.scalar.copy(out=votes[:], in_=acc_of[n][:])
+            nc.scalar.copy(out=votes[:], in_=acc_of[n][:, 0:COLS])
             nc.sync.dma_start(out=out_dram[:, n, :], in_=votes[:])
 
         last = len(units) - 1
@@ -211,27 +237,32 @@ def tile_transforming_k_kernel(tc, inputs, transform_mat, out):
         load_x(2)
         load_pair(2, 0)
         regroup_w(*units[0])
+        quantise_w(*units[0])
         for u in range(3):
             sort_x(*units[u])
-            turn_x(*units[u])
-            if u > 0:
-                copy_x(*units[u - 1])
+        turn_x(*units[0])
+        turn_x(*units[1])
+        copy_x(*units[0])
+        turn_x(*units[2])
+        copy_x(*units[1])
 
-        for u, (n, c) in enumerate(units):
+        for u, (n, c) in enumerate(units[:last]):
             if u == 0:
                 continue
-            if u < last:
-                regroup_w(n, c)
-                copy_x(*units[u + 1])
-            else:
-                regroup_w(n, c, LAST_VECTOR_GROUPS, 2)
+            regroup_w(n, c)
+            copy_x(*units[u + 1])
             if u == 1:
                 quantise_x(*units[0])
             quantise_x(n, c)
-            quantise_w(*units[u - 1], 1)
+            if u > 1:
+                quantise_w(*units[u - 1])
             multiply(*units[u - 1])
-            if u + 2 <= last:
+            if u == 3:
+                for next_c in range(1, CLASSES):
+                    sort_x(n + 1, next_c)
+            elif u + 2 <= last and u not in (4, 5):
                 sort_x(*units[u + 2])
+            if u + 2 <= last:
                 turn_x(*units[u + 2])
             if u == 3:
                 load_pair(2, 2)
@@ -239,9 +270,23 @@ def tile_transforming_k_kernel(tc, inputs, transform_mat, out):
             if u == 5:
                 load_pair(3, 0)
                 load_single(3, 2)
-                load_single(3, 3, 2)
+                load_single(3, 3, LAST_PARTS)
             if c == 1 and n > 0:
                 store(n - 1)
-        quantise_w(*units[last], 2)
-        multiply(*units[last])
-        store(CAPS_IN - 1)
+
+        n, c = units[last]
+        weight_tiles((n, c))
+        part_words = GROUPS * PART_COLS
+        votes = results.tile([P, COLS], F32)
+        for part, ms in enumerate(m_parts(LAST_PARTS)):
+            words = slice(part * part_words * PACK, (part + 1) * part_words * PACK)
+            regroup_runs(n, c, ms, w_grouped_of[(n, c)][:, words], LAST_VECTOR_GROUPS)
+        quantise_x(n, c)
+        quantise_w(*units[last - 1])
+        multiply(*units[last - 1])
+        for part in range(LAST_PARTS):
+            cols = slice(part * PART_COLS, (part + 1) * PART_COLS)
+            quantise_columns((n, c), part * part_words, part_words)
+            multiply_columns(n, c, last_acc_of[part], part * part_words, PART_COLS, PART_COLS)
+            nc.scalar.copy(out=votes[:, cols], in_=last_acc_of[part][:, 0:PART_COLS])
+            nc.sync.dma_start(out=out_dram[:, n, cols], in_=votes[:, cols])

from contextlib import ExitStack

import concourse.mybir as mybir
from concourse.masks import make_identity

BF16 = mybir.dt.bfloat16
F32 = mybir.dt.float32
U32 = mybir.dt.uint32
U8 = mybir.dt.uint8
FP8X4 = mybir.dt.float8_e4m3fn_x4

P = 128
BATCH = 128
CAPS_IN = 4
CAPS_OUT = 16
D_IN = 8192
D_OUT = 16
COLS = CAPS_OUT * D_OUT

PACK = 4
GROUPS = 4
RUN = GROUPS * PACK
HALVES = 2
CLASSES = 4
CHUNKS = D_IN // (CLASSES * HALVES * RUN)
VECTOR_GROUPS = 2
SCALAR_HEAVY = ((0, 3), (2, 1))
LAST_VECTOR_GROUPS = 3
LAST_PARTS = 2
PART_COLS = COLS // LAST_PARTS
BANK = 512
RUN_ELEMS = RUN * D_OUT

FLOPS = 2 * BATCH * CAPS_IN * D_IN * COLS


def tile_transforming_k_kernel(tc, inputs, transform_mat, out):
    nc = tc.nc
    assert CHUNKS * HALVES == P

    x_dram = inputs.rearrange("b n i one -> b n (i one)")
    w_dram = transform_mat.rearrange("one n m (j s) o uno -> (one n) j m (s o uno)", j=CHUNKS)
    out_dram = out.rearrange("b n m o one -> b n (m o one)")

    units = [(n, c) for n in range(CAPS_IN) for c in range(CLASSES)]

    with ExitStack() as ctx:
        keep = ctx.enter_context(tc.tile_pool(name="keep", bufs=1))
        x_in = ctx.enter_context(tc.tile_pool(name="x_in", bufs=3))
        x_rough = ctx.enter_context(tc.tile_pool(name="x_rough", bufs=6))
        x_mid = ctx.enter_context(tc.tile_pool(name="x_mid", bufs=3))
        x_mx = ctx.enter_context(tc.tile_pool(name="x_mx", bufs=2))
        w_pairs = ctx.enter_context(tc.tile_pool(name="w_pairs", bufs=4))
        w_singles = ctx.enter_context(tc.tile_pool(name="w_singles", bufs=2))
        w_mid = ctx.enter_context(tc.tile_pool(name="w_mid", bufs=3))
        results = ctx.enter_context(tc.tile_pool(name="results", bufs=2))
        psum_t = ctx.enter_context(tc.psum_pool(name="psum_t", bufs=4))
        psum_acc = ctx.enter_context(tc.psum_pool(name="psum_acc", bufs=2))
        psum_last = ctx.enter_context(tc.psum_pool(name="psum_last", bufs=LAST_PARTS))
        ctx.enter_context(tc.manual_schedule())

        ident = keep.tile([P, P], F32)
        make_identity(nc, ident[:])

        first_copy = keep.tile([P, 1], F32)
        nc.scalar.copy(out=first_copy[:], in_=ident[:, 0:1])

        x_mx_of = {}
        x_rows_of = {}
        x_grouped_of = {}
        w_rows_of = {}
        w_grouped_of = {}
        w_mx_of = {}
        last_acc_of = {}
        acc_of = {}

        def load_x(n):
            x_rows = x_in.tile([P, D_IN], BF16)
            nc.sync.dma_start(out=x_rows[:], in_=x_dram[:, n, :])
            x_rows_of[n] = x_rows

        def m_parts(parts):
            return [slice(i * CAPS_OUT // parts, (i + 1) * CAPS_OUT // parts) for i in range(parts)]

        def load_runs(n, parity, run, runs, out, ms=slice(0, CAPS_OUT)):
            nc.sync.dma_start(
                out=out[parity:P:HALVES, ms],
                in_=w_dram[n, :, ms, run * RUN_ELEMS : (run + runs) * RUN_ELEMS],
            )

        def load_single(n, c, parts=1):
            w_rows = w_singles.tile([P, CAPS_OUT * RUN_ELEMS], BF16)
            by_m = w_rows[:].rearrange("p (m e) -> p m e", m=CAPS_OUT)
            for ms in m_parts(parts):
                for parity in range(HALVES):
                    load_runs(n, parity, 2 * c + (c + parity) % 2, 1, by_m, ms)
            w_rows_of[(n, c)] = by_m

        def load_pair(n, c):
            w_rows = w_pairs.tile([P, CAPS_OUT * 2 * RUN_ELEMS], BF16)
            by_m = w_rows[:].rearrange("p (m e) -> p m e", m=CAPS_OUT)
            load_runs(n, 0, 2 * c, 1, by_m[:, :, :RUN_ELEMS])
            load_runs(n, 1, 2 * c + 1, 2, by_m)
            load_runs(n, 0, 2 * c + 3, 1, by_m[:, :, RUN_ELEMS:])
            w_rows_of[(n, c)] = by_m[:, :, :RUN_ELEMS]
            w_rows_of[(n, c + 1)] = by_m[:, :, RUN_ELEMS:]

        x_sorted_of = {}
        x_banks_of = {}

        def sort_x(n, c):
            by_class = x_rows_of[n][:].rearrange(
                "b (j c h g t) -> b c g j h t", c=CLASSES, h=HALVES, g=GROUPS, t=PACK
            )[:, c]
            if c % 2 == 1:
                by_class = by_class[:, :, :, ::-1, :]
            x_sorted = x_rough.tile([P, P * RUN], BF16)
            nc.vector.tensor_copy(
                out=x_sorted[:].rearrange("b (g j h t) -> b g j h t", g=GROUPS, h=HALVES, t=PACK),
                in_=by_class,
            )
            x_sorted_of[(n, c)] = x_sorted

        def turn_x(n, c):
            x_words = x_sorted_of[(n, c)][:].bitcast(F32).rearrange(
                "b (g p u) -> b g u p", g=GROUPS, u=2
            )
            banks = []
            for first_g in range(0, GROUPS, 2):
                xt = psum_t.tile([P, 4 * BATCH], F32)
                for w in range(4):
                    nc.tensor.transpose(
                        xt[:, w * BATCH : (w + 1) * BATCH],
                        x_words[:, first_g + w // 2, w % 2],
                        ident[:],
                    )
                banks.append(xt)
            x_banks_of[(n, c)] = banks

        def copy_x(n, c):
            x_grouped = x_mid.tile([P, GROUPS * BATCH * PACK], BF16, align_bytes=64)
            x_grouped_of[(n, c)] = x_grouped
            grouped_words = x_grouped[:].bitcast(F32).rearrange(
                "p (g b u) -> p g b u", g=GROUPS, b=BATCH
            )
            for i, xt in enumerate(x_banks_of[(n, c)]):
                nc.scalar.copy(
                    out=grouped_words[:, 2 * i : 2 * i + 2],
                    in_=xt[:].rearrange("p (g u b) -> p g b u", g=2, u=2),
                )

        def quantise_x(n, c):
            if c == 0:
                x_codes = x_mx.tile([P, CLASSES, GROUPS * BATCH], U32, align_bytes=64)
                x_scales = x_mx.tile([P, CLASSES, GROUPS * BATCH], U8, align_bytes=64)
                x_mx_of[n] = (x_codes, x_scales)
            x_codes, x_scales = x_mx_of[n]
            nc.vector.quantize_mx(
                out=x_codes[:, c].bitcast(FP8X4), scales=x_scales[:, c], in_=x_grouped_of[(n, c)][:]
            )

        def regroup_runs(n, c, ms, out, vector_groups):
            src = w_rows_of[(n, c)][:, ms].rearrange("p m (g t q i) -> p g m q t i", g=GROUPS, t=PACK, i=4)
            dst = out.rearrange("p (g m q i t) -> p g m q t i", g=GROUPS, q=D_OUT // 4, i=4, t=PACK)
            for g in range(GROUPS):
                if g < vector_groups:
                    nc.vector.tensor_copy(out=dst[:, g], in_=src[:, g])
                else:
                    nc.scalar.copy(out=dst[:, g], in_=src[:, g])

        def quantise_columns(key, first, columns):
            w_codes, w_scales = w_mx_of[key]
            share = slice(first, first + columns)
            nc.vector.quantize_mx(
                out=w_codes[:, share].bitcast(FP8X4),
                scales=w_scales[:, share],
                in_=w_grouped_of[key][:, first * PACK : (first + columns) * PACK],
            )

        def weight_tiles(key):
            w_grouped = w_mid.tile([P, GROUPS * COLS * PACK], BF16, align_bytes=64)
            w_codes = w_mid.tile([P, GROUPS * COLS], U32, align_bytes=64)
            w_scales = w_mid.tile([P, GROUPS * COLS], U8, align_bytes=64)
            w_grouped_of[key] = w_grouped
            w_mx_of[key] = (w_codes, w_scales)

        def regroup_w(n, c):
            weight_tiles((n, c))
            vector_groups = 1 if (n, c) in SCALAR_HEAVY else VECTOR_GROUPS
            regroup_runs(n, c, slice(0, CAPS_OUT), w_grouped_of[(n, c)][:], vector_groups)

        def quantise_w(n, c):
            quantise_columns((n, c), 0, GROUPS * COLS)

        def multiply_columns(n, c, acc, first, step, columns):
            w_codes, w_scales = w_mx_of[(n, c)]
            x_codes, x_scales = x_mx_of[n]
            for g in range(GROUPS):
                b_cols = slice(g * BATCH, (g + 1) * BATCH)
                w_cols = slice(first + g * step, first + g * step + columns)
                nc.tensor.matmul_mx(
                    out=acc[:, 0:columns],
                    lhsT=x_codes[:, c, b_cols].bitcast(FP8X4),
                    lhsT_scale=x_scales[:, c, b_cols],
                    rhs=w_codes[:, w_cols].bitcast(FP8X4),
                    rhs_scale=w_scales[:, w_cols],
                    start=(c == 0 and g == 0),
                    stop=(c == CLASSES - 1 and g == GROUPS - 1),
                )

        def multiply(n, c):
            if n < CAPS_IN - 1:
                if c == 0:
                    acc = psum_acc.tile([P, BANK], F32)
                    acc_of[n] = acc
                multiply_columns(n, c, acc_of[n], 0, COLS, COLS)
            else:
                for part in range(LAST_PARTS):
                    if c == 0:
                        last_acc = psum_last.tile([P, BANK], F32)
                        last_acc_of[part] = last_acc
                    multiply_columns(n, c, last_acc_of[part], part * PART_COLS, COLS, PART_COLS)

        def store(n):
            votes = results.tile([P, COLS], F32)
            nc.scalar.copy(out=votes[:], in_=acc_of[n][:, 0:COLS])
            nc.sync.dma_start(out=out_dram[:, n, :], in_=votes[:])

        last = len(units) - 1
        load_single(0, 0)
        load_x(0)
        load_single(0, 1)
        load_pair(0, 2)
        load_x(1)
        load_pair(1, 0)
        load_pair(1, 2)
        load_x(2)
        load_pair(2, 0)
        regroup_w(*units[0])
        quantise_w(*units[0])
        for u in range(3):
            sort_x(*units[u])
        turn_x(*units[0])
        turn_x(*units[1])
        copy_x(*units[0])
        turn_x(*units[2])
        copy_x(*units[1])

        for u, (n, c) in enumerate(units[:last]):
            if u == 0:
                continue
            regroup_w(n, c)
            copy_x(*units[u + 1])
            if u == 1:
                quantise_x(*units[0])
            quantise_x(n, c)
            if u > 1:
                quantise_w(*units[u - 1])
            multiply(*units[u - 1])
            if u == 3:
                for next_c in range(1, CLASSES):
                    sort_x(n + 1, next_c)
            elif u + 2 <= last and u not in (4, 5):
                sort_x(*units[u + 2])
            if u + 2 <= last:
                turn_x(*units[u + 2])
            if u == 3:
                load_pair(2, 2)
                load_x(3)
            if u == 5:
                load_pair(3, 0)
                load_single(3, 2)
                load_single(3, 3, LAST_PARTS)
            if c == 1 and n > 0:
                store(n - 1)

        n, c = units[last]
        weight_tiles((n, c))
        part_words = GROUPS * PART_COLS
        votes = results.tile([P, COLS], F32)
        for part, ms in enumerate(m_parts(LAST_PARTS)):
            words = slice(part * part_words * PACK, (part + 1) * part_words * PACK)
            regroup_runs(n, c, ms, w_grouped_of[(n, c)][:, words], LAST_VECTOR_GROUPS)
        quantise_x(n, c)
        quantise_w(*units[last - 1])
        multiply(*units[last - 1])
        for part in range(LAST_PARTS):
            cols = slice(part * PART_COLS, (part + 1) * PART_COLS)
            quantise_columns((n, c), part * part_words, part_words)
            multiply_columns(n, c, last_acc_of[part], part * part_words, PART_COLS, PART_COLS)
            nc.scalar.copy(out=votes[:, cols], in_=last_acc_of[part][:, 0:PART_COLS])
            nc.sync.dma_start(out=out_dram[:, n, cols], in_=votes[:, cols])
